import numpy as np
import ml_dtypes


def mxq(x, axis, fmt="e4m3"):
    dtype, down = {"e4m3": (ml_dtypes.float8_e4m3fn, 7), "e5m2": (ml_dtypes.float8_e5m2, 14)}[fmt]
    v = np.moveaxis(np.asarray(x, np.float32).astype(ml_dtypes.bfloat16).astype(np.float64), axis, -1)
    blocks = v.reshape(v.shape[:-1] + (-1, 32))
    amax = np.abs(blocks).max(-1, keepdims=True)
    byte = np.maximum(np.where(amax > 0, np.frexp(amax)[1] - 1 + 127, 0) - down, 1)
    scale = np.exp2(byte - 127.0)
    codes = (blocks / scale).astype(np.float32).astype(dtype).astype(np.float64)
    return np.moveaxis((codes * scale).reshape(v.shape), -1, axis)


WIDE = False


def mx_kscale(k):
    if not WIDE:
        return np.ones(k)
    levels = np.array([20, -20, 10, -10, 0])
    a = np.random.permutation(np.resize(levels, k // 512 * 4)).reshape(k // 512, 4)
    idx = np.arange(k)
    return np.exp2(a[idx // 512, idx % 128 // 32])


BF16 = ml_dtypes.bfloat16


def bf(x):
    return np.asarray(x, np.float32).astype(BF16)


def f64(x):
    return np.asarray(x).astype(np.float64)


B, C, PPC, D, R = 2048, 256, 8, 1024, 8
P = C * PPC
GAP = 1e-3


def setup_inputs():
    sc = mx_kscale(P)[::PPC]
    sp = np.repeat(sc, PPC)
    top = np.max(sc)
    u = np.random.standard_normal((R, D))
    q = 0.5 / np.sqrt(D)
    x0 = bf((np.random.standard_normal((B, R)) @ u + np.random.standard_normal((B, D))) * q)
    p0 = bf((np.random.standard_normal((P, R)) @ u + np.random.standard_normal((P, D))) * q)
    xf, pf = f64(x0), f64(p0)
    sq = np.sum(xf * xf, axis=1, keepdims=True) + np.sum(pf * pf, axis=1)[None, :] - 2.0 * (xf @ pf.T)
    d = np.sqrt(np.maximum(sq, 0.0))
    g = np.random.standard_normal((B, C)) * np.exp2(np.random.randint(-12, 1, (B, 1))) * 16.0
    ds = np.sort(d.reshape(B, C, PPC), axis=2)
    g = g * ((ds[:, :, 1] - ds[:, :, 0]) > GAP)
    return {"x": bf(xf / top), "prototypes": bf(pf / sp[:, None]), "dists": np.asarray(d, np.float32),
            "grad_out": bf(g * sc[None, :])}


def reference(x, prototypes, dists, grad_out):
    x, prototypes, g = f64(x), f64(prototypes), f64(grad_out)
    d3 = f64(dists).reshape(B, C, PPC)
    near = d3 == np.min(d3, axis=2, keepdims=True)
    a = np.where(near, g[:, :, None] / d3, 0.0).reshape(B, P)
    r = np.sum(a, axis=1, keepdims=True)
    return (mxq(a, 1, "e5m2") @ mxq(prototypes, 0, "e4m3")) - r * x

@@ -1,0 +1,193 @@
+from contextlib import ExitStack
+
+import concourse.mybir as mybir
+from concourse.masks import make_identity
+
+F32 = mybir.dt.float32
+BF16 = mybir.dt.bfloat16
+U32 = mybir.dt.uint32
+U8 = mybir.dt.uint8
+E5M2_X4 = mybir.dt.float8_e5m2_x4
+E4M3_X4 = mybir.dt.float8_e4m3fn_x4
+ALU = mybir.AluOpType
+ACT = mybir.ActivationFunctionType
+
+P = 128
+B = 2048
+K = 2048
+D = 1024
+PPC = 8
+C = K // PPC
+HALF_C = C // 2
+PACK = 4
+K_PASS = P * PACK
+PASSES = K // K_PASS
+N_TILE = 512
+N_TILES = D // N_TILE
+TOKEN_TILES = B // P
+K_BLOCKS = K // P
+BLOCKS_PER_BANK = 8
+PREFETCH = 2
+LAG = PASSES - 1
+
+FLOPS = 2 * B * K * D
+
+
+def tile_lvq_t_v_kernel(tc, x, prototypes, dists, grad_out, out):
+    nc = tc.nc
+
+    d_view = dists.rearrange("(p i) k -> p i k", i=TOKEN_TILES)
+    g_view = grad_out.rearrange("(p i) c -> p i c", i=TOKEN_TILES)
+    x_view = x.rearrange("(p i) d -> p i d", i=TOKEN_TILES)
+    out_view = out.rearrange("(p i) d -> p i d", i=TOKEN_TILES)
+    proto_view = prototypes.rearrange("(s t p) d -> s p t d", t=PACK, p=P)
+
+    with ExitStack() as stack:
+        keep = stack.enter_context(tc.tile_pool(name="keep", bufs=1))
+        proto_stage = stack.enter_context(tc.tile_pool(name="proto_stage", bufs=2))
+        dist_pool = stack.enter_context(tc.tile_pool(name="dist", bufs=PREFETCH + 2))
+        per_class = stack.enter_context(tc.tile_pool(name="per_class", bufs=3))
+        wide = stack.enter_context(tc.tile_pool(name="wide", bufs=3))
+        mx = stack.enter_context(tc.tile_pool(name="mx", bufs=LAG + 3))
+        result_pool = stack.enter_context(tc.tile_pool(name="result", bufs=3))
+        transposed_pool = stack.enter_context(tc.psum_pool(name="transposed", bufs=4))
+        acc_pool = stack.enter_context(tc.psum_pool(name="acc", bufs=4))
+
+        ident = keep.tile([P, P], BF16)
+        make_identity(nc, ident[:])
+        g_sb = keep.tile([P, TOKEN_TILES, C], BF16)
+        p_words = keep.tile([P, PASSES, D], U32, align_bytes=64)
+        p_scales = keep.tile([P, PASSES, D], U8, align_bytes=64)
+
+        def load_dists(i):
+            d_sb = dist_pool.tile([P, K], F32, name="d_sb")
+            nc.sync.dma_start(out=d_sb[:], in_=d_view[:, i, :])
+            return d_sb
+
+        def quantise_prototypes(s):
+            raw = proto_stage.tile([P, PACK, D], BF16, name="raw")
+            nc.sync.dma_start(out=raw[:], in_=proto_view[s])
+            grouped = proto_stage.tile([P, D, PACK], BF16, name="p_grouped", align_bytes=64)
+            for n in range(N_TILES):
+                cols = slice(n * N_TILE, (n + 1) * N_TILE)
+                nc.scalar.copy(out=grouped[:, cols, :], in_=raw[:, :, cols].rearrange("p t d -> p d t"))
+            nc.vector.quantize_mx(
+                out=p_words[:, s, :].bitcast(E4M3_X4),
+                scales=p_scales[:, s, :],
+                in_=grouped[:].rearrange("p d t -> p (d t)"),
+            )
+
+        def make_a(i, d_sb):
+            m = per_class.tile([P, C], F32, name="m")
+            nc.vector.tensor_reduce(
+                out=m[:].rearrange("p (X h) -> p h X", h=2),
+                in_=d_sb[:].rearrange("p (h X j) -> p h X j", h=2, j=PPC),
+                axis=mybir.AxisListType.X,
+                op=ALU.min,
+            )
+            rsqrt_m = per_class.tile([P, C], F32, name="rsqrt_m")
+            nc.scalar.activation(out=rsqrt_m[:], in_=m[:], func=ACT.Abs_reciprocal_sqrt)
+            guess = per_class.tile([P, C], F32, name="guess")
+            nc.scalar.activation(out=guess[:], in_=rsqrt_m[:], func=ACT.Square)
+            m_guess = per_class.tile([P, C], F32, name="m_guess")
+            nc.vector.tensor_tensor(out=m_guess[:], in0=m[:], in1=guess[:], op=ALU.mult)
+            neg_w_guess = per_class.tile([P, C], F32, name="neg_w_guess")
+            nc.vector.scalar_tensor_tensor(
+                out=neg_w_guess[:].rearrange("p (X h) -> p X h", h=2),
+                in0=g_sb[:, i, :].rearrange("p (h X) -> p X h", h=2),
+                scalar=-1.0,
+                in1=guess[:].rearrange("p (X h) -> p X h", h=2),
+                op0=ALU.mult,
+                op1=ALU.mult,
+            )
+            w = per_class.tile([P, C], F32, name="w")
+            nc.vector.scalar_tensor_tensor(
+                out=w[:], in0=m_guess[:], scalar=2.0, in1=neg_w_guess[:], op0=ALU.subtract, op1=ALU.mult
+            )
+            w_bf = per_class.tile([P, C], BF16, name="w_bf")
+            r = per_class.tile([P, 1], F32, name="r")
+            nc.scalar.activation(out=w_bf[:], in_=w[:], func=ACT.Copy, accum_out=r[:])
+            neg_r = mx.tile([P, 1], F32, name="neg_r")
+            nc.scalar.mul(out=neg_r[:], in_=r[:], mul=-1.0)
+
+            near = wide.tile([P, K], BF16, name="near")
+            nc.vector.tensor_tensor(
+                out=near[:].rearrange("p (X j h) -> p X j h", j=PPC, h=2),
+                in0=d_sb[:].rearrange("p (h X j) -> p X j h", h=2, j=PPC),
+                in1=m[:].rearrange("p (X o h) -> p X o h", o=1, h=2).to_broadcast([P, HALF_C, PPC, 2]),
+                op=ALU.is_equal,
+            )
+            a = wide.tile([P, K], BF16, name="a")
+            nc.vector.tensor_tensor(
+                out=a[:].rearrange("p (X j h) -> p X j h", j=PPC, h=2),
+                in0=near[:].rearrange("p (X j h) -> p X j h", j=PPC, h=2),
+                in1=w_bf[:].rearrange("p (X o h) -> p X o h", o=1, h=2).to_broadcast([P, HALF_C, PPC, 2]),
+                op=ALU.mult,
+            )
+            return a, neg_r
+
+        def quantise_a(a):
+            a_blocks = a[:].rearrange("p (u q h) -> p h u q", u=K_BLOCKS // 2, h=2)
+            grouped = wide.tile([P, PASSES, P, PACK], BF16, name="a_grouped", align_bytes=64)
+            passes_per_bank = BLOCKS_PER_BANK // PACK
+            for bank in range(K_BLOCKS // BLOCKS_PER_BANK):
+                a_t = transposed_pool.tile([P, BLOCKS_PER_BANK, P], BF16, name="a_t")
+                for u in range(BLOCKS_PER_BANK):
+                    nc.tensor.transpose(out=a_t[:, u, :], in_=a_blocks[:, bank, u, :], identity=ident[:])
+                nc.scalar.copy(
+                    out=grouped[:, bank * passes_per_bank : (bank + 1) * passes_per_bank, :, :],
+                    in_=a_t[:].rearrange("p (s t) b -> p s b t", t=PACK),
+                )
+            a_words = mx.tile([P, PASSES * P], U32, name="a_words", align_bytes=64)
+            a_scales = mx.tile([P, PASSES * P], U8, name="a_scales", align_bytes=64)
+            nc.vector.quantize_mx(
+                out=a_words[:].bitcast(E5M2_X4),
+                scales=a_scales[:],
+                in_=grouped[:].rearrange("p s b t -> p (s b t)"),
+            )
+            return a_words, a_scales
+
+        def multiply_and_store(i, a_words, a_scales, neg_r):
+            x_sb = result_pool.tile([P, D], BF16, name="x_sb")
+            nc.sync.dma_start(out=x_sb[:], in_=x_view[:, i, :])
+            result = result_pool.tile([P, D], F32, name="result")
+            for n in range(N_TILES):
+                cols = slice(n * N_TILE, (n + 1) * N_TILE)
+                acc = acc_pool.tile([P, N_TILE], F32, name="acc")
+                for s in range(PASSES):
+                    tokens = slice(s * P, (s + 1) * P)
+                    nc.tensor.matmul_mx(
+                        out=acc[:],
+                        lhsT=a_words[:, tokens].bitcast(E5M2_X4),
+                        lhsT_scale=a_scales[:, tokens],
+                        rhs=p_words[:, s, cols].bitcast(E4M3_X4),
+                        rhs_scale=p_scales[:, s, cols],
+                        start=(s == 0),
+                        stop=(s == PASSES - 1),
+                    )
+                nc.vector.scalar_tensor_tensor(
+                    out=result[:, cols],
+                    in0=x_sb[:, cols],
+                    scalar=neg_r[:, 0:1],
+                    in1=acc[:],
+                    op0=ALU.mult,
+                    op1=ALU.add,
+                )
+            nc.sync.dma_start(out=out_view[:, i, :], in_=result[:])
+
+        d_tiles = {}
+        for i in range(PREFETCH):
+            d_tiles[i] = load_dists(i)
+        nc.sync.dma_start(out=g_sb[:], in_=g_view)
+        quantised = {}
+        for i in range(TOKEN_TILES + LAG):
+            if i + PREFETCH < TOKEN_TILES:
+                d_tiles[i + PREFETCH] = load_dists(i + PREFETCH)
+            if i < TOKEN_TILES:
+                a, neg_r = make_a(i, d_tiles[i])
+                if i < PASSES:
+                    quantise_prototypes(i)
+                a_words, a_scales = quantise_a(a)
+                quantised[i] = (a_words, a_scales, neg_r)
+            if i >= LAG:
+                multiply_and_store(i - LAG, *quantised[i - LAG])

@@ -19,14 +19,15 @@ D = 1024
 PPC = 8
 C = K // PPC
 HALF_C = C // 2
+PAIRS = PPC // 2
 PACK = 4
 K_PASS = P * PACK
 PASSES = K // K_PASS
 N_TILE = 512
 N_TILES = D // N_TILE
 TOKEN_TILES = B // P
-K_BLOCKS = K // P
-BLOCKS_PER_BANK = 8
+WORD_BLOCKS = K // (2 * P)
+BLOCKS_PER_BANK = 4
 PREFETCH = 2
 LAG = PASSES - 1
 
@@ -40,7 +41,7 @@ def tile_lvq_t_v_kernel(tc, x, prototypes, dists, grad_out, out):
     g_view = grad_out.rearrange("(p i) c -> p i c", i=TOKEN_TILES)
     x_view = x.rearrange("(p i) d -> p i d", i=TOKEN_TILES)
     out_view = out.rearrange("(p i) d -> p i d", i=TOKEN_TILES)
-    proto_view = prototypes.rearrange("(s t p) d -> s p t d", t=PACK, p=P)
+    proto_view = prototypes.rearrange("(s u p e) d -> s p u e d", u=2, p=P, e=2)
 
     with ExitStack() as stack:
         keep = stack.enter_context(tc.tile_pool(name="keep", bufs=1))
@@ -53,7 +54,7 @@ def tile_lvq_t_v_kernel(tc, x, prototypes, dists, grad_out, out):
         transposed_pool = stack.enter_context(tc.psum_pool(name="transposed", bufs=4))
         acc_pool = stack.enter_context(tc.psum_pool(name="acc", bufs=4))
 
-        ident = keep.tile([P, P], BF16)
+        ident = keep.tile([P, P], F32)
         make_identity(nc, ident[:])
         g_sb = keep.tile([P, TOKEN_TILES, C], BF16)
         p_words = keep.tile([P, PASSES, D], U32, align_bytes=64)
@@ -66,7 +67,7 @@ def tile_lvq_t_v_kernel(tc, x, prototypes, dists, grad_out, out):
 
         def quantise_prototypes(s):
             raw = proto_stage.tile([P, PACK, D], BF16, name="raw")
-            nc.sync.dma_start(out=raw[:], in_=proto_view[s])
+            nc.sync.dma_start(out=raw[:].rearrange("p (u e) d -> p u e d", u=2), in_=proto_view[s])
             grouped = proto_stage.tile([P, D, PACK], BF16, name="p_grouped", align_bytes=64)
             for n in range(N_TILES):
                 cols = slice(n * N_TILE, (n + 1) * N_TILE)
@@ -77,14 +78,26 @@ def tile_lvq_t_v_kernel(tc, x, prototypes, dists, grad_out, out):
                 in_=grouped[:].rearrange("p d t -> p (d t)"),
             )
 
+        def spread(per_class_tile):
+            return per_class_tile[:].rearrange("p (h X o) -> p X h o", h=2, o=1).to_broadcast([P, HALF_C, 2, 2])
+
+        def over_pairs(spread_tile):
+            return (
+                spread_tile[:]
+                .rearrange("p (X o h e) -> p X o h e", o=1, h=2, e=2)
+                .to_broadcast([P, HALF_C, PAIRS, 2, 2])
+            )
+
+        def woven(wide_tile):
+            return wide_tile[:].rearrange("p (X q h e) -> p X q h e", q=PAIRS, h=2, e=2)
+
         def make_a(i, d_sb):
             m = per_class.tile([P, C], F32, name="m")
             nc.vector.tensor_reduce(
-                out=m[:].rearrange("p (X h) -> p h X", h=2),
-                in_=d_sb[:].rearrange("p (h X j) -> p h X j", h=2, j=PPC),
-                axis=mybir.AxisListType.X,
-                op=ALU.min,
+                out=m[:], in_=d_sb[:].rearrange("p (c j) -> p c j", j=PPC), axis=mybir.AxisListType.X, op=ALU.min
             )
+            m_spread = per_class.tile([P, 2 * C], F32, name="m_spread")
+            nc.scalar.copy(out=m_spread[:].rearrange("p (X h e) -> p X h e", h=2, e=2), in_=spread(m))
             rsqrt_m = per_class.tile([P, C], F32, name="rsqrt_m")
             nc.scalar.activation(out=rsqrt_m[:], in_=m[:], func=ACT.Abs_reciprocal_sqrt)
             guess = per_class.tile([P, C], F32, name="guess")
@@ -93,58 +106,50 @@ def tile_lvq_t_v_kernel(tc, x, prototypes, dists, grad_out, out):
             nc.vector.tensor_tensor(out=m_guess[:], in0=m[:], in1=guess[:], op=ALU.mult)
             neg_w_guess = per_class.tile([P, C], F32, name="neg_w_guess")
             nc.vector.scalar_tensor_tensor(
-                out=neg_w_guess[:].rearrange("p (X h) -> p X h", h=2),
-                in0=g_sb[:, i, :].rearrange("p (h X) -> p X h", h=2),
-                scalar=-1.0,
-                in1=guess[:].rearrange("p (X h) -> p X h", h=2),
-                op0=ALU.mult,
-                op1=ALU.mult,
+                out=neg_w_guess[:], in0=g_sb[:, i, :], scalar=-1.0, in1=guess[:], op0=ALU.mult, op1=ALU.mult
             )
             w = per_class.tile([P, C], F32, name="w")
             nc.vector.scalar_tensor_tensor(
                 out=w[:], in0=m_guess[:], scalar=2.0, in1=neg_w_guess[:], op0=ALU.subtract, op1=ALU.mult
             )
-            w_bf = per_class.tile([P, C], BF16, name="w_bf")
-            r = per_class.tile([P, 1], F32, name="r")
-            nc.scalar.activation(out=w_bf[:], in_=w[:], func=ACT.Copy, accum_out=r[:])
+            w_spread = per_class.tile([P, 2 * C], BF16, name="w_spread")
+            twice_r = per_class.tile([P, 1], F32, name="twice_r")
+            nc.scalar.activation(
+                out=w_spread[:].rearrange("p (X h e) -> p X h e", h=2, e=2),
+                in_=spread(w),
+                func=ACT.Copy,
+                accum_out=twice_r[:],
+            )
             neg_r = mx.tile([P, 1], F32, name="neg_r")
-            nc.scalar.mul(out=neg_r[:], in_=r[:], mul=-1.0)
+            nc.scalar.mul(out=neg_r[:], in_=twice_r[:], mul=-0.5)
 
             near = wide.tile([P, K], BF16, name="near")
             nc.vector.tensor_tensor(
-                out=near[:].rearrange("p (X j h) -> p X j h", j=PPC, h=2),
-                in0=d_sb[:].rearrange("p (h X j) -> p X j h", h=2, j=PPC),
-                in1=m[:].rearrange("p (X o h) -> p X o h", o=1, h=2).to_broadcast([P, HALF_C, PPC, 2]),
+                out=woven(near),
+                in0=d_sb[:].rearrange("p (h X q e) -> p X q h e", h=2, q=PAIRS, e=2),
+                in1=over_pairs(m_spread),
                 op=ALU.is_equal,
             )
             a = wide.tile([P, K], BF16, name="a")
-            nc.vector.tensor_tensor(
-                out=a[:].rearrange("p (X j h) -> p X j h", j=PPC, h=2),
-                in0=near[:].rearrange("p (X j h) -> p X j h", j=PPC, h=2),
-                in1=w_bf[:].rearrange("p (X o h) -> p X o h", o=1, h=2).to_broadcast([P, HALF_C, PPC, 2]),
-                op=ALU.mult,
-            )
+            nc.vector.tensor_tensor(out=woven(a), in0=woven(near), in1=over_pairs(w_spread), op=ALU.mult)
             return a, neg_r
 
         def quantise_a(a):
-            a_blocks = a[:].rearrange("p (u q h) -> p h u q", u=K_BLOCKS // 2, h=2)
-            grouped = wide.tile([P, PASSES, P, PACK], BF16, name="a_grouped", align_bytes=64)
-            passes_per_bank = BLOCKS_PER_BANK // PACK
-            for bank in range(K_BLOCKS // BLOCKS_PER_BANK):
-                a_t = transposed_pool.tile([P, BLOCKS_PER_BANK, P], BF16, name="a_t")
-                for u in range(BLOCKS_PER_BANK):
-                    nc.tensor.transpose(out=a_t[:, u, :], in_=a_blocks[:, bank, u, :], identity=ident[:])
+            a_blocks = a[:].bitcast(F32).rearrange("p (v y h) -> p h v y", v=WORD_BLOCKS // 2, h=2)
+            grouped = wide.tile([P, PASSES * P * PACK], BF16, name="a_grouped", align_bytes=64)
+            grouped_words = grouped[:].bitcast(F32).rearrange("p (s b u) -> p s b u", b=P, u=2)
+            passes_per_bank = BLOCKS_PER_BANK // 2
+            for bank in range(WORD_BLOCKS // BLOCKS_PER_BANK):
+                a_t = transposed_pool.tile([P, BLOCKS_PER_BANK, P], F32, name="a_t")
+                for v in range(BLOCKS_PER_BANK):
+                    nc.tensor.transpose(out=a_t[:, v, :], in_=a_blocks[:, bank, v, :], identity=ident[:])
                 nc.scalar.copy(
-                    out=grouped[:, bank * passes_per_bank : (bank + 1) * passes_per_bank, :, :],
-                    in_=a_t[:].rearrange("p (s t) b -> p s b t", t=PACK),
+                    out=grouped_words[:, bank * passes_per_bank : (bank + 1) * passes_per_bank, :, :],
+                    in_=a_t[:].rearrange("p (s u) b -> p s b u", u=2),
                 )
             a_words = mx.tile([P, PASSES * P], U32, name="a_words", align_bytes=64)
             a_scales = mx.tile([P, PASSES * P], U8, name="a_scales", align_bytes=64)
-            nc.vector.quantize_mx(
-                out=a_words[:].bitcast(E5M2_X4),
-                scales=a_scales[:],
-                in_=grouped[:].rearrange("p s b t -> p (s b t)"),
-            )
+            nc.vector.quantize_mx(out=a_words[:].bitcast(E5M2_X4), scales=a_scales[:], in_=grouped[:])
             return a_words, a_scales
 
         def multiply_and_store(i, a_words, a_scales, neg_r):

@@ -103,15 +103,15 @@ def tile_lvq_t_v_kernel(tc, x, prototypes, dists, grad_out, out):
             guess = per_class.tile([P, C], F32, name="guess")
             nc.scalar.activation(out=guess[:], in_=rsqrt_m[:], func=ACT.Square)
             m_guess = per_class.tile([P, C], F32, name="m_guess")
-            nc.vector.tensor_tensor(out=m_guess[:], in0=m[:], in1=guess[:], op=ALU.mult)
-            neg_w_guess = per_class.tile([P, C], F32, name="neg_w_guess")
-            nc.vector.scalar_tensor_tensor(
-                out=neg_w_guess[:], in0=g_sb[:, i, :], scalar=-1.0, in1=guess[:], op0=ALU.mult, op1=ALU.mult
+            nc.gpsimd.tensor_tensor(out=m_guess[:], in0=m[:], in1=guess[:], op=ALU.mult)
+            w_guess = per_class.tile([P, C], F32, name="w_guess")
+            nc.gpsimd.tensor_tensor(out=w_guess[:], in0=g_sb[:, i, :], in1=guess[:], op=ALU.mult)
+            correction = per_class.tile([P, C], F32, name="correction")
+            nc.gpsimd.tensor_scalar(
+                out=correction[:], in0=m_guess[:], scalar1=-1.0, scalar2=2.0, op0=ALU.mult, op1=ALU.add
             )
             w = per_class.tile([P, C], F32, name="w")
-            nc.vector.scalar_tensor_tensor(
-                out=w[:], in0=m_guess[:], scalar=2.0, in1=neg_w_guess[:], op0=ALU.subtract, op1=ALU.mult
-            )
+            nc.gpsimd.tensor_tensor(out=w[:], in0=w_guess[:], in1=correction[:], op=ALU.mult)
             w_spread = per_class.tile([P, 2 * C], BF16, name="w_spread")
             twice_r = per_class.tile([P, 1], F32, name="twice_r")
             nc.scalar.activation(

@@ -29,7 +29,8 @@ TOKEN_TILES = B // P
 WORD_BLOCKS = K // (2 * P)
 BLOCKS_PER_BANK = 4
 PREFETCH = 2
-LAG = PASSES - 1
+G_CHUNK = 4
+SCALE_LAG = 4
 
 FLOPS = 2 * B * K * D
 
@@ -45,38 +46,22 @@ def tile_lvq_t_v_kernel(tc, x, prototypes, dists, grad_out, out):
 
     with ExitStack() as stack:
         keep = stack.enter_context(tc.tile_pool(name="keep", bufs=1))
-        proto_stage = stack.enter_context(tc.tile_pool(name="proto_stage", bufs=2))
+        proto_pool = stack.enter_context(tc.tile_pool(name="proto", bufs=3))
         dist_pool = stack.enter_context(tc.tile_pool(name="dist", bufs=PREFETCH + 2))
-        per_class = stack.enter_context(tc.tile_pool(name="per_class", bufs=3))
-        wide = stack.enter_context(tc.tile_pool(name="wide", bufs=3))
-        mx = stack.enter_context(tc.tile_pool(name="mx", bufs=LAG + 3))
-        result_pool = stack.enter_context(tc.tile_pool(name="result", bufs=3))
+        waiting = stack.enter_context(tc.tile_pool(name="waiting", bufs=SCALE_LAG + 2))
+        short = stack.enter_context(tc.tile_pool(name="short", bufs=3))
+        neg_r_pool = stack.enter_context(tc.tile_pool(name="neg_r", bufs=5))
+        result_pool = stack.enter_context(tc.tile_pool(name="result", bufs=4))
         transposed_pool = stack.enter_context(tc.psum_pool(name="transposed", bufs=4))
         acc_pool = stack.enter_context(tc.psum_pool(name="acc", bufs=4))
+        stack.enter_context(tc.manual_schedule())
 
         ident = keep.tile([P, P], F32)
         make_identity(nc, ident[:])
         g_sb = keep.tile([P, TOKEN_TILES, C], BF16)
         p_words = keep.tile([P, PASSES, D], U32, align_bytes=64)
         p_scales = keep.tile([P, PASSES, D], U8, align_bytes=64)
-
-        def load_dists(i):
-            d_sb = dist_pool.tile([P, K], F32, name="d_sb")
-            nc.sync.dma_start(out=d_sb[:], in_=d_view[:, i, :])
-            return d_sb
-
-        def quantise_prototypes(s):
-            raw = proto_stage.tile([P, PACK, D], BF16, name="raw")
-            nc.sync.dma_start(out=raw[:].rearrange("p (u e) d -> p u e d", u=2), in_=proto_view[s])
-            grouped = proto_stage.tile([P, D, PACK], BF16, name="p_grouped", align_bytes=64)
-            for n in range(N_TILES):
-                cols = slice(n * N_TILE, (n + 1) * N_TILE)
-                nc.scalar.copy(out=grouped[:, cols, :], in_=raw[:, :, cols].rearrange("p t d -> p d t"))
-            nc.vector.quantize_mx(
-                out=p_words[:, s, :].bitcast(E4M3_X4),
-                scales=p_scales[:, s, :],
-                in_=grouped[:].rearrange("p d t -> p (d t)"),
-            )
+        tiles = {}
 
         def spread(per_class_tile):
             return per_class_tile[:].rearrange("p (h X o) -> p X h o", h=2, o=1).to_broadcast([P, HALF_C, 2, 2])
@@ -91,71 +76,126 @@ def tile_lvq_t_v_kernel(tc, x, prototypes, dists, grad_out, out):
         def woven(wide_tile):
             return wide_tile[:].rearrange("p (X q h e) -> p X q h e", q=PAIRS, h=2, e=2)
 
-        def make_a(i, d_sb):
-            m = per_class.tile([P, C], F32, name="m")
-            nc.vector.tensor_reduce(
-                out=m[:], in_=d_sb[:].rearrange("p (c j) -> p c j", j=PPC), axis=mybir.AxisListType.X, op=ALU.min
-            )
-            m_spread = per_class.tile([P, 2 * C], F32, name="m_spread")
-            nc.scalar.copy(out=m_spread[:].rearrange("p (X h e) -> p X h e", h=2, e=2), in_=spread(m))
-            rsqrt_m = per_class.tile([P, C], F32, name="rsqrt_m")
-            nc.scalar.activation(out=rsqrt_m[:], in_=m[:], func=ACT.Abs_reciprocal_sqrt)
-            guess = per_class.tile([P, C], F32, name="guess")
-            nc.scalar.activation(out=guess[:], in_=rsqrt_m[:], func=ACT.Square)
-            m_guess = per_class.tile([P, C], F32, name="m_guess")
-            nc.gpsimd.tensor_tensor(out=m_guess[:], in0=m[:], in1=guess[:], op=ALU.mult)
-            w_guess = per_class.tile([P, C], F32, name="w_guess")
-            nc.gpsimd.tensor_tensor(out=w_guess[:], in0=g_sb[:, i, :], in1=guess[:], op=ALU.mult)
-            correction = per_class.tile([P, C], F32, name="correction")
-            nc.gpsimd.tensor_scalar(
-                out=correction[:], in0=m_guess[:], scalar1=-1.0, scalar2=2.0, op0=ALU.mult, op1=ALU.add
-            )
-            w = per_class.tile([P, C], F32, name="w")
-            nc.gpsimd.tensor_tensor(out=w[:], in0=w_guess[:], in1=correction[:], op=ALU.mult)
-            w_spread = per_class.tile([P, 2 * C], BF16, name="w_spread")
-            twice_r = per_class.tile([P, 1], F32, name="twice_r")
-            nc.scalar.activation(
-                out=w_spread[:].rearrange("p (X h e) -> p X h e", h=2, e=2),
-                in_=spread(w),
-                func=ACT.Copy,
-                accum_out=twice_r[:],
-            )
-            neg_r = mx.tile([P, 1], F32, name="neg_r")
-            nc.scalar.mul(out=neg_r[:], in_=twice_r[:], mul=-0.5)
+        def load_dists(i):
+            d_sb = dist_pool.tile([P, K], F32, name="d_sb")
+            nc.sync.dma_start(out=d_sb[:], in_=d_view[:, i, :])
+            tiles["d", i] = d_sb
 
-            near = wide.tile([P, K], BF16, name="near")
+        def load_prototypes(s):
+            raw = proto_pool.tile([P, PACK, D], BF16, name="raw")
+            nc.sync.dma_start(out=raw[:].rearrange("p (u e) d -> p u e d", u=2), in_=proto_view[s])
+            tiles["raw", s] = raw
+
+        def regroup_prototypes(s):
+            grouped = proto_pool.tile([P, D, PACK], BF16, name="p_grouped", align_bytes=64)
+            for n in range(N_TILES):
+                cols = slice(n * N_TILE, (n + 1) * N_TILE)
+                nc.scalar.copy(out=grouped[:, cols, :], in_=tiles["raw", s][:, :, cols].rearrange("p t d -> p d t"))
+            tiles["p_grouped", s] = grouped
+
+        def quantise_prototypes(s):
+            nc.vector.quantize_mx(
+                out=p_words[:, s, :].bitcast(E4M3_X4),
+                scales=p_scales[:, s, :],
+                in_=tiles["p_grouped", s][:].rearrange("p d t -> p (d t)"),
+            )
+
+        def find_minima(i):
+            m = short.tile([P, C], F32, name="m")
+            nc.vector.tensor_reduce(
+                out=m[:],
+                in_=tiles["d", i][:].rearrange("p (c j) -> p c j", j=PPC),
+                axis=mybir.AxisListType.X,
+                op=ALU.min,
+            )
+            m_spread = short.tile([P, 2 * C], F32, name="m_spread")
+            nc.scalar.copy(out=m_spread[:].rearrange("p (X h e) -> p X h e", h=2, e=2), in_=spread(m))
+            tiles["m", i] = m
+            tiles["m_spread", i] = m_spread
+
+        def compare(i):
+            near = waiting.tile([P, K], BF16, name="near")
             nc.vector.tensor_tensor(
                 out=woven(near),
-                in0=d_sb[:].rearrange("p (h X q e) -> p X q h e", h=2, q=PAIRS, e=2),
-                in1=over_pairs(m_spread),
+                in0=tiles["d", i][:].rearrange("p (h X q e) -> p X q h e", h=2, q=PAIRS, e=2),
+                in1=over_pairs(tiles["m_spread", i]),
                 op=ALU.is_equal,
             )
-            a = wide.tile([P, K], BF16, name="a")
-            nc.vector.tensor_tensor(out=woven(a), in0=woven(near), in1=over_pairs(w_spread), op=ALU.mult)
-            return a, neg_r
+            tiles["near", i] = near
 
-        def quantise_a(a):
-            a_blocks = a[:].bitcast(F32).rearrange("p (v y h) -> p h v y", v=WORD_BLOCKS // 2, h=2)
-            grouped = wide.tile([P, PASSES * P * PACK], BF16, name="a_grouped", align_bytes=64)
-            grouped_words = grouped[:].bitcast(F32).rearrange("p (s b u) -> p s b u", b=P, u=2)
-            passes_per_bank = BLOCKS_PER_BANK // 2
+        def guess_reciprocal(i):
+            rsqrt_m = short.tile([P, C], F32, name="rsqrt_m")
+            nc.scalar.activation(out=rsqrt_m[:], in_=tiles["m", i][:], func=ACT.Abs_reciprocal_sqrt)
+            guess = short.tile([P, C], F32, name="guess")
+            nc.scalar.activation(out=guess[:], in_=rsqrt_m[:], func=ACT.Square)
+            tiles["guess", i] = guess
+
+        def newton_products(i):
+            m_guess = waiting.tile([P, C], F32, name="m_guess")
+            nc.gpsimd.tensor_tensor(out=m_guess[:], in0=tiles["m", i][:], in1=tiles["guess", i][:], op=ALU.mult)
+            w_guess = waiting.tile([P, C], F32, name="w_guess")
+            nc.gpsimd.tensor_tensor(out=w_guess[:], in0=g_sb[:, i, :], in1=tiles["guess", i][:], op=ALU.mult)
+            tiles["m_guess", i] = m_guess
+            tiles["w_guess", i] = w_guess
+
+        def newton_finish(i):
+            neg_w = short.tile([P, C], F32, name="neg_w")
+            nc.vector.scalar_tensor_tensor(
+                out=neg_w[:],
+                in0=tiles["m_guess", i][:],
+                scalar=2.0,
+                in1=tiles["w_guess", i][:],
+                op0=ALU.subtract,
+                op1=ALU.mult,
+            )
+            w_spread = short.tile([P, 2 * C], BF16, name="w_spread")
+            twice_r = short.tile([P, 1], F32, name="twice_r")
+            nc.scalar.activation(
+                out=w_spread[:].rearrange("p (X h e) -> p X h e", h=2, e=2),
+                in_=spread(neg_w),
+                func=ACT.Copy,
+                scale=-1.0,
+                accum_out=twice_r[:],
+            )
+            neg_r = neg_r_pool.tile([P, 1], F32, name="neg_r")
+            nc.scalar.mul(out=neg_r[:], in_=twice_r[:], mul=-0.5)
+            tiles["w_spread", i] = w_spread
+            tiles["neg_r", i] = neg_r
+
+        def scale_and_transpose(i):
+            a = short.tile([P, K], BF16, name="a")
+            nc.vector.tensor_tensor(
+                out=woven(a), in0=woven(tiles["near", i]), in1=over_pairs(tiles["w_spread", i]), op=ALU.mult
+            )
+            a_blocks = a[:].bitcast(F32).rearrange("p (v y h) -> p h v y", v=BLOCKS_PER_BANK, h=2)
             for bank in range(WORD_BLOCKS // BLOCKS_PER_BANK):
                 a_t = transposed_pool.tile([P, BLOCKS_PER_BANK, P], F32, name="a_t")
                 for v in range(BLOCKS_PER_BANK):
                     nc.tensor.transpose(out=a_t[:, v, :], in_=a_blocks[:, bank, v, :], identity=ident[:])
+                tiles["a_t", i, bank] = a_t
+
+        def copy_out(i):
+            grouped = short.tile([P, PASSES * P * PACK], BF16, name="a_grouped", align_bytes=64)
+            grouped_words = grouped[:].bitcast(F32).rearrange("p (s b u) -> p s b u", b=P, u=2)
+            passes_per_bank = BLOCKS_PER_BANK // 2
+            for bank in range(WORD_BLOCKS // BLOCKS_PER_BANK):
                 nc.scalar.copy(
                     out=grouped_words[:, bank * passes_per_bank : (bank + 1) * passes_per_bank, :, :],
-                    in_=a_t[:].rearrange("p (s u) b -> p s b u", u=2),
+                    in_=tiles["a_t", i, bank][:].rearrange("p (s u) b -> p s b u", u=2),
                 )
-            a_words = mx.tile([P, PASSES * P], U32, name="a_words", align_bytes=64)
-            a_scales = mx.tile([P, PASSES * P], U8, name="a_scales", align_bytes=64)
-            nc.vector.quantize_mx(out=a_words[:].bitcast(E5M2_X4), scales=a_scales[:], in_=grouped[:])
-            return a_words, a_scales
+            tiles["a_grouped", i] = grouped
 
-        def multiply_and_store(i, a_words, a_scales, neg_r):
-            x_sb = result_pool.tile([P, D], BF16, name="x_sb")
+        def quantise_a(i):
+            a_words = short.tile([P, PASSES * P], U32, name="a_words", align_bytes=64)
+            a_scales = short.tile([P, PASSES * P], U8, name="a_scales", align_bytes=64)
+            nc.vector.quantize_mx(out=a_words[:].bitcast(E5M2_X4), scales=a_scales[:], in_=tiles["a_grouped", i][:])
+            tiles["a_words", i] = a_words
+            tiles["a_scales", i] = a_scales
+
+        def multiply(i):
+            x_sb = short.tile([P, D], BF16, name="x_sb")
             nc.sync.dma_start(out=x_sb[:], in_=x_view[:, i, :])
-            result = result_pool.tile([P, D], F32, name="result")
+            tiles["x", i] = x_sb
             for n in range(N_TILES):
                 cols = slice(n * N_TILE, (n + 1) * N_TILE)
                 acc = acc_pool.tile([P, N_TILE], F32, name="acc")
@@ -163,36 +203,59 @@ def tile_lvq_t_v_kernel(tc, x, prototypes, dists, grad_out, out):
                     tokens = slice(s * P, (s + 1) * P)
                     nc.tensor.matmul_mx(
                         out=acc[:],
-                        lhsT=a_words[:, tokens].bitcast(E5M2_X4),
-                        lhsT_scale=a_scales[:, tokens],
+                        lhsT=tiles["a_words", i][:, tokens].bitcast(E5M2_X4),
+                        lhsT_scale=tiles["a_scales", i][:, tokens],
                         rhs=p_words[:, s, cols].bitcast(E4M3_X4),
                         rhs_scale=p_scales[:, s, cols],
                         start=(s == 0),
                         stop=(s == PASSES - 1),
                     )
+                tiles["acc", i, n] = acc
+
+        def subtract_and_store(i):
+            for n in range(N_TILES):
+                cols = slice(n * N_TILE, (n + 1) * N_TILE)
+                result = result_pool.tile([P, N_TILE], F32, name="result")
                 nc.vector.scalar_tensor_tensor(
-                    out=result[:, cols],
-                    in0=x_sb[:, cols],
-                    scalar=neg_r[:, 0:1],
-                    in1=acc[:],
+                    out=result[:],
+                    in0=tiles["x", i][:, cols],
+                    scalar=tiles["neg_r", i][:, 0:1],
+                    in1=tiles["acc", i, n][:],
                     op0=ALU.mult,
                     op1=ALU.add,
                 )
-            nc.sync.dma_start(out=out_view[:, i, :], in_=result[:])
+                nc.sync.dma_start(out=out_view[:, i, cols], in_=result[:])
 
-        d_tiles = {}
+        def is_tile(i):
+            return 0 <= i < TOKEN_TILES
+
         for i in range(PREFETCH):
-            d_tiles[i] = load_dists(i)
-        nc.sync.dma_start(out=g_sb[:], in_=g_view)
-        quantised = {}
-        for i in range(TOKEN_TILES + LAG):
-            if i + PREFETCH < TOKEN_TILES:
-                d_tiles[i + PREFETCH] = load_dists(i + PREFETCH)
-            if i < TOKEN_TILES:
-                a, neg_r = make_a(i, d_tiles[i])
-                if i < PASSES:
-                    quantise_prototypes(i)
-                a_words, a_scales = quantise_a(a)
-                quantised[i] = (a_words, a_scales, neg_r)
-            if i >= LAG:
-                multiply_and_store(i - LAG, *quantised[i - LAG])
+            load_dists(i)
+        for i in range(TOKEN_TILES + SCALE_LAG + 3):
+            j = i - SCALE_LAG
+            if i < PASSES:
+                load_prototypes(i)
+            if is_tile(i + PREFETCH):
+                load_dists(i + PREFETCH)
+            if is_tile(i) and i % G_CHUNK == 0:
+                nc.sync.dma_start(out=g_sb[:, i : i + G_CHUNK, :], in_=g_view[:, i : i + G_CHUNK, :])
+            if is_tile(i):
+                find_minima(i)
+                guess_reciprocal(i)
+                newton_products(i)
+            if i < PASSES:
+                regroup_prototypes(i)
+            if is_tile(i - 1):
+                compare(i - 1)
+            if is_tile(j):
+                newton_finish(j)
+            if is_tile(j - 1):
+                scale_and_transpose(j - 1)
+                copy_out(j - 1)
+            if 0 <= i - 3 < PASSES:
+                quantise_prototypes(i - 3)
+            if is_tile(j - 2):
+                quantise_a(j - 2)
+                multiply(j - 2)
+            if is_tile(j - 3):
+                subtract_and_store(j - 3)

@@ -18,19 +18,15 @@ K = 2048
 D = 1024
 PPC = 8
 C = K // PPC
-HALF_C = C // 2
-PAIRS = PPC // 2
 PACK = 4
 K_PASS = P * PACK
 PASSES = K // K_PASS
 N_TILE = 512
 N_TILES = D // N_TILE
 TOKEN_TILES = B // P
-WORD_BLOCKS = K // (2 * P)
-BLOCKS_PER_BANK = 4
 PREFETCH = 2
 G_CHUNK = 4
-SCALE_LAG = 4
+STEEP = 2.0**60
 
 FLOPS = 2 * B * K * D
 
@@ -42,18 +38,19 @@ def tile_lvq_t_v_kernel(tc, x, prototypes, dists, grad_out, out):
     g_view = grad_out.rearrange("(p i) c -> p i c", i=TOKEN_TILES)
     x_view = x.rearrange("(p i) d -> p i d", i=TOKEN_TILES)
     out_view = out.rearrange("(p i) d -> p i d", i=TOKEN_TILES)
-    proto_view = prototypes.rearrange("(s u p e) d -> s p u e d", u=2, p=P, e=2)
+    proto_view = prototypes.rearrange("(s p t) d -> s p t d", p=P, t=PACK)
 
     with ExitStack() as stack:
         keep = stack.enter_context(tc.tile_pool(name="keep", bufs=1))
-        proto_pool = stack.enter_context(tc.tile_pool(name="proto", bufs=3))
-        dist_pool = stack.enter_context(tc.tile_pool(name="dist", bufs=PREFETCH + 2))
-        waiting = stack.enter_context(tc.tile_pool(name="waiting", bufs=SCALE_LAG + 2))
+        proto_pool = stack.enter_context(tc.tile_pool(name="proto", bufs=2))
+        dist_pool = stack.enter_context(tc.tile_pool(name="dist", bufs=PREFETCH + 3))
         short = stack.enter_context(tc.tile_pool(name="short", bufs=3))
-        neg_r_pool = stack.enter_context(tc.tile_pool(name="neg_r", bufs=5))
+        x_pool = stack.enter_context(tc.tile_pool(name="x_pool", bufs=4))
+        neg_r_pool = stack.enter_context(tc.tile_pool(name="neg_r", bufs=6))
         result_pool = stack.enter_context(tc.tile_pool(name="result", bufs=4))
-        transposed_pool = stack.enter_context(tc.psum_pool(name="transposed", bufs=4))
-        acc_pool = stack.enter_context(tc.psum_pool(name="acc", bufs=4))
+        diff_pool = stack.enter_context(tc.psum_pool(name="diff", bufs=4))
+        w_t_pool = stack.enter_context(tc.psum_pool(name="w_t", bufs=1))
+        acc_pool = stack.enter_context(tc.psum_pool(name="acc", bufs=3))
         stack.enter_context(tc.manual_schedule())
 
         ident = keep.tile([P, P], F32)
@@ -63,34 +60,32 @@ def tile_lvq_t_v_kernel(tc, x, prototypes, dists, grad_out, out):
         p_scales = keep.tile([P, PASSES, D], U8, align_bytes=64)
         tiles = {}
 
-        def spread(per_class_tile):
-            return per_class_tile[:].rearrange("p (h X o) -> p X h o", h=2, o=1).to_broadcast([P, HALF_C, 2, 2])
-
-        def over_pairs(spread_tile):
-            return (
-                spread_tile[:]
-                .rearrange("p (X o h e) -> p X o h e", o=1, h=2, e=2)
-                .to_broadcast([P, HALF_C, PAIRS, 2, 2])
-            )
-
-        def woven(wide_tile):
-            return wide_tile[:].rearrange("p (X q h e) -> p X q h e", q=PAIRS, h=2, e=2)
+        def repeated(per_class_tile, times):
+            return per_class_tile[:].rearrange("p (c o) -> p c o", o=1).to_broadcast([P, C, times])
 
         def load_dists(i):
             d_sb = dist_pool.tile([P, K], F32, name="d_sb")
             nc.sync.dma_start(out=d_sb[:], in_=d_view[:, i, :])
             tiles["d", i] = d_sb
 
+        def load_grad_out(i):
+            nc.sync.dma_start(out=g_sb[:, i : i + G_CHUNK, :], in_=g_view[:, i : i + G_CHUNK, :])
+
+        def load_x(i):
+            x_sb = x_pool.tile([P, D], BF16, name="x_sb")
+            nc.sync.dma_start(out=x_sb[:], in_=x_view[:, i, :])
+            tiles["x", i] = x_sb
+
         def load_prototypes(s):
             raw = proto_pool.tile([P, PACK, D], BF16, name="raw")
-            nc.sync.dma_start(out=raw[:].rearrange("p (u e) d -> p u e d", u=2), in_=proto_view[s])
+            nc.sync.dma_start(out=raw[:], in_=proto_view[s])
             tiles["raw", s] = raw
 
         def regroup_prototypes(s):
             grouped = proto_pool.tile([P, D, PACK], BF16, name="p_grouped", align_bytes=64)
             for n in range(N_TILES):
                 cols = slice(n * N_TILE, (n + 1) * N_TILE)
-                nc.scalar.copy(out=grouped[:, cols, :], in_=tiles["raw", s][:, :, cols].rearrange("p t d -> p d t"))
+                nc.vector.tensor_copy(out=grouped[:, cols, :], in_=tiles["raw", s][:, :, cols].rearrange("p t d -> p d t"))
             tiles["p_grouped", s] = grouped
 
         def quantise_prototypes(s):
@@ -108,20 +103,14 @@ def tile_lvq_t_v_kernel(tc, x, prototypes, dists, grad_out, out):
                 axis=mybir.AxisListType.X,
                 op=ALU.min,
             )
-            m_spread = short.tile([P, 2 * C], F32, name="m_spread")
-            nc.scalar.copy(out=m_spread[:].rearrange("p (X h e) -> p X h e", h=2, e=2), in_=spread(m))
             tiles["m", i] = m
-            tiles["m_spread", i] = m_spread
 
-        def compare(i):
-            near = waiting.tile([P, K], BF16, name="near")
-            nc.vector.tensor_tensor(
-                out=woven(near),
-                in0=tiles["d", i][:].rearrange("p (h X q e) -> p X q h e", h=2, q=PAIRS, e=2),
-                in1=over_pairs(tiles["m_spread", i]),
-                op=ALU.is_equal,
+        def negate_minima(i):
+            neg_m = short.tile([P, 2 * C], F32, name="neg_m")
+            nc.scalar.activation(
+                out=neg_m[:].rearrange("p (c v) -> p c v", v=2), in_=repeated(tiles["m", i], 2), func=ACT.Copy, scale=-1.0
             )
-            tiles["near", i] = near
+            tiles["neg_m", i] = neg_m
 
         def guess_reciprocal(i):
             rsqrt_m = short.tile([P, C], F32, name="rsqrt_m")
@@ -131,15 +120,16 @@ def tile_lvq_t_v_kernel(tc, x, prototypes, dists, grad_out, out):
             tiles["guess", i] = guess
 
         def newton_products(i):
-            m_guess = waiting.tile([P, C], F32, name="m_guess")
+            m_guess = short.tile([P, C], F32, name="m_guess")
             nc.gpsimd.tensor_tensor(out=m_guess[:], in0=tiles["m", i][:], in1=tiles["guess", i][:], op=ALU.mult)
-            w_guess = waiting.tile([P, C], F32, name="w_guess")
+            w_guess = short.tile([P, C], F32, name="w_guess")
             nc.gpsimd.tensor_tensor(out=w_guess[:], in0=g_sb[:, i, :], in1=tiles["guess", i][:], op=ALU.mult)
             tiles["m_guess", i] = m_guess
             tiles["w_guess", i] = w_guess
 
         def newton_finish(i):
             neg_w = short.tile([P, C], F32, name="neg_w")
+            neg_r = neg_r_pool.tile([P, 1], F32, name="neg_r")
             nc.vector.scalar_tensor_tensor(
                 out=neg_w[:],
                 in0=tiles["m_guess", i][:],
@@ -147,43 +137,67 @@ def tile_lvq_t_v_kernel(tc, x, prototypes, dists, grad_out, out):
                 in1=tiles["w_guess", i][:],
                 op0=ALU.subtract,
                 op1=ALU.mult,
+                accum_out=neg_r[:],
             )
-            w_spread = short.tile([P, 2 * C], BF16, name="w_spread")
-            twice_r = short.tile([P, 1], F32, name="twice_r")
-            nc.scalar.activation(
-                out=w_spread[:].rearrange("p (X h e) -> p X h e", h=2, e=2),
-                in_=spread(neg_w),
-                func=ACT.Copy,
-                scale=-1.0,
-                accum_out=twice_r[:],
-            )
-            neg_r = neg_r_pool.tile([P, 1], F32, name="neg_r")
-            nc.scalar.mul(out=neg_r[:], in_=twice_r[:], mul=-0.5)
-            tiles["w_spread", i] = w_spread
+            tiles["neg_w", i] = neg_w
             tiles["neg_r", i] = neg_r
 
-        def scale_and_transpose(i):
-            a = short.tile([P, K], BF16, name="a")
-            nc.vector.tensor_tensor(
-                out=woven(a), in0=woven(tiles["near", i]), in1=over_pairs(tiles["w_spread", i]), op=ALU.mult
+        def round_weights(i):
+            w_pairs = short.tile([P, 4 * C], BF16, name="w_pairs")
+            nc.scalar.activation(
+                out=w_pairs[:].rearrange("p (c f) -> p c f", f=4), in_=repeated(tiles["neg_w", i], 4), func=ACT.Copy, scale=-1.0
             )
-            a_blocks = a[:].bitcast(F32).rearrange("p (v y h) -> p h v y", v=BLOCKS_PER_BANK, h=2)
-            for bank in range(WORD_BLOCKS // BLOCKS_PER_BANK):
-                a_t = transposed_pool.tile([P, BLOCKS_PER_BANK, P], F32, name="a_t")
-                for v in range(BLOCKS_PER_BANK):
-                    nc.tensor.transpose(out=a_t[:, v, :], in_=a_blocks[:, bank, v, :], identity=ident[:])
-                tiles["a_t", i, bank] = a_t
+            tiles["w_pairs", i] = w_pairs
 
-        def copy_out(i):
-            grouped = short.tile([P, PASSES * P * PACK], BF16, name="a_grouped", align_bytes=64)
-            grouped_words = grouped[:].bitcast(F32).rearrange("p (s b u) -> p s b u", b=P, u=2)
-            passes_per_bank = BLOCKS_PER_BANK // 2
-            for bank in range(WORD_BLOCKS // BLOCKS_PER_BANK):
-                nc.scalar.copy(
-                    out=grouped_words[:, bank * passes_per_bank : (bank + 1) * passes_per_bank, :, :],
-                    in_=tiles["a_t", i, bank][:].rearrange("p (s u) b -> p s b u", u=2),
+        def transpose_differences(i, s):
+            diff = diff_pool.tile([P, PACK, P], F32, name="diff")
+            d_cols = tiles["d", i][:].rearrange("p (s q t) -> p s t q", s=PASSES, t=PACK)
+            for t in range(PACK):
+                nc.tensor.matmul(
+                    out=diff[:, t, :], lhsT=d_cols[:, s, t, :], rhs=ident[:], start=True, stop=False, is_transpose=True
                 )
-            tiles["a_grouped", i] = grouped
+                nc.tensor.matmul(
+                    out=diff[:, t, :],
+                    lhsT=tiles["neg_m", i][:, s * P : (s + 1) * P],
+                    rhs=ident[:],
+                    start=False,
+                    stop=True,
+                    is_transpose=True,
+                )
+            tiles["diff", i, s] = diff
+
+        def mark_nearest(i, s):
+            if s == 0:
+                tiles["near", i] = short.tile([P, PASSES, P, PACK], BF16, name="near")
+            nc.scalar.activation(
+                out=tiles["near", i][:, s, :, :],
+                in_=tiles["diff", i, s][:].rearrange("p t b -> p b t"),
+                func=ACT.Relu,
+                scale=-STEEP,
+                bias=1.0,
+            )
+
+        def transpose_weights(i):
+            w_t = w_t_pool.tile([P, PASSES, P], F32, name="w_t")
+            w_words = tiles["w_pairs", i][:].bitcast(F32)
+            for s in range(PASSES):
+                nc.tensor.transpose(out=w_t[:, s, :], in_=w_words[:, s * P : (s + 1) * P], identity=ident[:])
+            w_t_sb = short.tile([P, PASSES * P], F32, name="w_t_sb")
+            nc.scalar.copy(out=w_t_sb[:], in_=w_t[:].rearrange("p s b -> p (s b)"))
+            tiles["w_t_sb", i] = w_t_sb
+
+        def scale_nearest(i):
+            a_grouped = short.tile([P, PASSES * P * PACK], BF16, name="a_grouped", align_bytes=64)
+            nc.vector.tensor_tensor(
+                out=a_grouped[:].rearrange("p (n u e) -> p n u e", u=2, e=2),
+                in0=tiles["near", i][:].rearrange("p s b (u e) -> p (s b) u e", u=2),
+                in1=tiles["w_t_sb", i][:]
+                .bitcast(BF16)
+                .rearrange("p (n o e) -> p n o e", o=1, e=2)
+                .to_broadcast([P, PASSES * P, 2, 2]),
+                op=ALU.mult,
+            )
+            tiles["a_grouped", i] = a_grouped
 
         def quantise_a(i):
             a_words = short.tile([P, PASSES * P], U32, name="a_words", align_bytes=64)
@@ -193,9 +207,6 @@ def tile_lvq_t_v_kernel(tc, x, prototypes, dists, grad_out, out):
             tiles["a_scales", i] = a_scales
 
         def multiply(i):
-            x_sb = short.tile([P, D], BF16, name="x_sb")
-            nc.sync.dma_start(out=x_sb[:], in_=x_view[:, i, :])
-            tiles["x", i] = x_sb
             for n in range(N_TILES):
                 cols = slice(n * N_TILE, (n + 1) * N_TILE)
                 acc = acc_pool.tile([P, N_TILE], F32, name="acc")
@@ -229,33 +240,46 @@ def tile_lvq_t_v_kernel(tc, x, prototypes, dists, grad_out, out):
         def is_tile(i):
             return 0 <= i < TOKEN_TILES
 
-        for i in range(PREFETCH):
-            load_dists(i)
-        for i in range(TOKEN_TILES + SCALE_LAG + 3):
-            j = i - SCALE_LAG
-            if i < PASSES:
-                load_prototypes(i)
-            if is_tile(i + PREFETCH):
-                load_dists(i + PREFETCH)
-            if is_tile(i) and i % G_CHUNK == 0:
-                nc.sync.dma_start(out=g_sb[:, i : i + G_CHUNK, :], in_=g_view[:, i : i + G_CHUNK, :])
-            if is_tile(i):
-                find_minima(i)
-                guess_reciprocal(i)
-                newton_products(i)
-            if i < PASSES:
-                regroup_prototypes(i)
-            if is_tile(i - 1):
-                compare(i - 1)
-            if is_tile(j):
-                newton_finish(j)
-            if is_tile(j - 1):
-                scale_and_transpose(j - 1)
-                copy_out(j - 1)
-            if 0 <= i - 3 < PASSES:
-                quantise_prototypes(i - 3)
-            if is_tile(j - 2):
-                quantise_a(j - 2)
-                multiply(j - 2)
-            if is_tile(j - 3):
-                subtract_and_store(j - 3)
+        load_dists(0)
+        load_grad_out(0)
+        load_prototypes(0)
+        load_dists(1)
+        for r in range(TOKEN_TILES + 4):
+            if r + 1 < PASSES:
+                load_prototypes(r + 1)
+            if is_tile(r + PREFETCH):
+                load_dists(r + PREFETCH)
+            if is_tile(r + 1) and (r + 1) % G_CHUNK == 0:
+                load_grad_out(r + 1)
+            if is_tile(r - 2):
+                load_x(r - 2)
+            if is_tile(r - 1):
+                newton_finish(r - 1)
+                round_weights(r - 1)
+                transpose_differences(r - 1, 0)
+                transpose_differences(r - 1, 1)
+                mark_nearest(r - 1, 0)
+                mark_nearest(r - 1, 1)
+            if is_tile(r):
+                find_minima(r)
+                negate_minima(r)
+                guess_reciprocal(r)
+                newton_products(r)
+            if is_tile(r - 1):
+                transpose_differences(r - 1, 2)
+                transpose_differences(r - 1, 3)
+                mark_nearest(r - 1, 2)
+                mark_nearest(r - 1, 3)
+                transpose_weights(r - 1)
+            if r < PASSES:
+                regroup_prototypes(r)
+            if is_tile(r - 3):
+                quantise_a(r - 3)
+            if is_tile(r - 2):
+                scale_nearest(r - 2)
+            if is_tile(r - 4):
+                subtract_and_store(r - 4)
+            if r < PASSES:
+                quantise_prototypes(r)
+            if is_tile(r - 3):
+                multiply(r - 3)

@@ -244,18 +244,19 @@ def tile_lvq_t_v_kernel(tc, x, prototypes, dists, grad_out, out):
         load_grad_out(0)
         load_prototypes(0)
         load_dists(1)
-        for r in range(TOKEN_TILES + 4):
+        for r in range(TOKEN_TILES + 5):
             if r + 1 < PASSES:
                 load_prototypes(r + 1)
             if is_tile(r + PREFETCH):
                 load_dists(r + PREFETCH)
             if is_tile(r + 1) and (r + 1) % G_CHUNK == 0:
                 load_grad_out(r + 1)
+            if is_tile(r - 3):
+                load_x(r - 3)
             if is_tile(r - 2):
-                load_x(r - 2)
+                newton_finish(r - 2)
+                round_weights(r - 2)
             if is_tile(r - 1):
-                newton_finish(r - 1)
-                round_weights(r - 1)
                 transpose_differences(r - 1, 0)
                 transpose_differences(r - 1, 1)
                 mark_nearest(r - 1, 0)
@@ -270,16 +271,17 @@ def tile_lvq_t_v_kernel(tc, x, prototypes, dists, grad_out, out):
                 transpose_differences(r - 1, 3)
                 mark_nearest(r - 1, 2)
                 mark_nearest(r - 1, 3)
-                transpose_weights(r - 1)
+            if is_tile(r - 2):
+                transpose_weights(r - 2)
             if r < PASSES:
                 regroup_prototypes(r)
-            if is_tile(r - 3):
-                quantise_a(r - 3)
-            if is_tile(r - 2):
-                scale_nearest(r - 2)
             if is_tile(r - 4):
-                subtract_and_store(r - 4)
+                quantise_a(r - 4)
+            if is_tile(r - 3):
+                scale_nearest(r - 3)
+            if is_tile(r - 5):
+                subtract_and_store(r - 5)
             if r < PASSES:
                 quantise_prototypes(r)
-            if is_tile(r - 3):
-                multiply(r - 3)
+            if is_tile(r - 4):
+                multiply(r - 4)

@@ -27,6 +27,7 @@ TOKEN_TILES = B // P
 PREFETCH = 2
 G_CHUNK = 4
 STEEP = 2.0**60
+VECTOR_PASS = 3
 
 FLOPS = 2 * B * K * D
 
@@ -166,6 +167,33 @@ def tile_lvq_t_v_kernel(tc, x, prototypes, dists, grad_out, out):
                 )
             tiles["diff", i, s] = diff
 
+        def compare_in_token_order(i, s):
+            near_rows = short.tile([P, K_PASS], BF16, name="near_rows")
+            classes = K_PASS // PPC
+            nc.vector.tensor_tensor(
+                out=near_rows[:].rearrange("p (c j) -> p c j", j=PPC),
+                in0=tiles["d", i][:, s * K_PASS : (s + 1) * K_PASS].rearrange("p (c j) -> p c j", j=PPC),
+                in1=tiles["m", i][:, s * classes : (s + 1) * classes]
+                .rearrange("p (c o) -> p c o", o=1)
+                .to_broadcast([P, classes, PPC]),
+                op=ALU.is_equal,
+            )
+            tiles["near_rows", i] = near_rows
+
+        def transpose_word_pairs(i, s):
+            pairs = diff_pool.tile([P, 2, P], F32, name="diff")
+            words = tiles["near_rows", i][:].bitcast(F32).rearrange("p (q u) -> p u q", u=2)
+            for u in range(2):
+                nc.tensor.transpose(out=pairs[:, u, :], in_=words[:, u, :], identity=ident[:])
+            tiles["pairs", i, s] = pairs
+
+        def copy_word_pairs(i, s):
+            near_words = tiles["near", i][:].rearrange("p s b t -> p (s b t)").bitcast(F32)
+            nc.scalar.copy(
+                out=near_words.rearrange("p (s b u) -> p s b u", s=PASSES, u=2)[:, s, :, :],
+                in_=tiles["pairs", i, s][:].rearrange("p u b -> p b u"),
+            )
+
         def mark_nearest(i, s):
             if s == 0:
                 tiles["near", i] = short.tile([P, PASSES, P, PACK], BF16, name="near")
@@ -263,14 +291,20 @@ def tile_lvq_t_v_kernel(tc, x, prototypes, dists, grad_out, out):
                 mark_nearest(r - 1, 1)
             if is_tile(r):
                 find_minima(r)
+                if r >= PASSES:
+                    compare_in_token_order(r, VECTOR_PASS)
                 negate_minima(r)
                 guess_reciprocal(r)
                 newton_products(r)
             if is_tile(r - 1):
                 transpose_differences(r - 1, 2)
-                transpose_differences(r - 1, 3)
                 mark_nearest(r - 1, 2)
-                mark_nearest(r - 1, 3)
+                if r - 1 >= PASSES:
+                    transpose_word_pairs(r - 1, VECTOR_PASS)
+                    copy_word_pairs(r - 1, VECTOR_PASS)
+                else:
+                    transpose_differences(r - 1, VECTOR_PASS)
+                    mark_nearest(r - 1, VECTOR_PASS)
             if is_tile(r - 2):
                 transpose_weights(r - 2)
             if r < PASSES:

@@ -61,12 +61,16 @@ def tile_lvq_t_v_kernel(tc, x, prototypes, dists, grad_out, out):
         p_scales = keep.tile([P, PASSES, D], U8, align_bytes=64)
         tiles = {}
 
-        def repeated(per_class_tile, times):
-            return per_class_tile[:].rearrange("p (c o) -> p c o", o=1).to_broadcast([P, C, times])
+        def repeated(per_class, times):
+            return per_class.rearrange("p (c o) -> p c o", o=1).to_broadcast([P, per_class.shape[1], times])
 
-        def load_dists(i):
+        def column_pieces(width, pieces):
+            return [slice(j * width // pieces, (j + 1) * width // pieces) for j in range(pieces)]
+
+        def load_dists(i, pieces=1):
             d_sb = dist_pool.tile([P, K], F32, name="d_sb")
-            nc.sync.dma_start(out=d_sb[:], in_=d_view[:, i, :])
+            for cols in column_pieces(K, pieces):
+                nc.sync.dma_start(out=d_sb[:, cols], in_=d_view[:, i, cols])
             tiles["d", i] = d_sb
 
         def load_grad_out(i):
@@ -79,7 +83,8 @@ def tile_lvq_t_v_kernel(tc, x, prototypes, dists, grad_out, out):
 
         def load_prototypes(s):
             raw = proto_pool.tile([P, PACK, D], BF16, name="raw")
-            nc.sync.dma_start(out=raw[:], in_=proto_view[s])
+            for cols in column_pieces(D, N_TILES):
+                nc.sync.dma_start(out=raw[:, :, cols], in_=proto_view[s][:, :, cols])
             tiles["raw", s] = raw
 
         def regroup_prototypes(s):
@@ -96,21 +101,23 @@ def tile_lvq_t_v_kernel(tc, x, prototypes, dists, grad_out, out):
                 in_=tiles["p_grouped", s][:].rearrange("p d t -> p (d t)"),
             )
 
-        def find_minima(i):
+        def find_minima(i, pieces=1):
             m = short.tile([P, C], F32, name="m")
-            nc.vector.tensor_reduce(
-                out=m[:],
-                in_=tiles["d", i][:].rearrange("p (c j) -> p c j", j=PPC),
-                axis=mybir.AxisListType.X,
-                op=ALU.min,
-            )
-            tiles["m", i] = m
-
-        def negate_minima(i):
             neg_m = short.tile([P, 2 * C], F32, name="neg_m")
-            nc.scalar.activation(
-                out=neg_m[:].rearrange("p (c v) -> p c v", v=2), in_=repeated(tiles["m", i], 2), func=ACT.Copy, scale=-1.0
-            )
+            for classes in column_pieces(C, pieces):
+                nc.vector.tensor_reduce(
+                    out=m[:, classes],
+                    in_=tiles["d", i][:].rearrange("p (c j) -> p c j", j=PPC)[:, classes, :],
+                    axis=mybir.AxisListType.X,
+                    op=ALU.min,
+                )
+                nc.scalar.activation(
+                    out=neg_m[:].rearrange("p (c v) -> p c v", v=2)[:, classes, :],
+                    in_=repeated(m[:, classes], 2),
+                    func=ACT.Copy,
+                    scale=-1.0,
+                )
+            tiles["m", i] = m
             tiles["neg_m", i] = neg_m
 
         def guess_reciprocal(i):
@@ -130,7 +137,6 @@ def tile_lvq_t_v_kernel(tc, x, prototypes, dists, grad_out, out):
 
         def newton_finish(i):
             neg_w = short.tile([P, C], F32, name="neg_w")
-            neg_r = neg_r_pool.tile([P, 1], F32, name="neg_r")
             nc.vector.scalar_tensor_tensor(
                 out=neg_w[:],
                 in0=tiles["m_guess", i][:],
@@ -138,17 +144,23 @@ def tile_lvq_t_v_kernel(tc, x, prototypes, dists, grad_out, out):
                 in1=tiles["w_guess", i][:],
                 op0=ALU.subtract,
                 op1=ALU.mult,
-                accum_out=neg_r[:],
             )
             tiles["neg_w", i] = neg_w
-            tiles["neg_r", i] = neg_r
 
         def round_weights(i):
             w_pairs = short.tile([P, 4 * C], BF16, name="w_pairs")
+            four_r = short.tile([P, 1], F32, name="four_r")
             nc.scalar.activation(
-                out=w_pairs[:].rearrange("p (c f) -> p c f", f=4), in_=repeated(tiles["neg_w", i], 4), func=ACT.Copy, scale=-1.0
+                out=w_pairs[:].rearrange("p (c f) -> p c f", f=4),
+                in_=repeated(tiles["neg_w", i][:], 4),
+                func=ACT.Copy,
+                scale=-1.0,
+                accum_out=four_r[:],
             )
+            neg_r = neg_r_pool.tile([P, 1], F32, name="neg_r")
+            nc.scalar.mul(out=neg_r[:], in_=four_r[:], mul=-0.25)
             tiles["w_pairs", i] = w_pairs
+            tiles["neg_r", i] = neg_r
 
         def transpose_differences(i, s):
             diff = diff_pool.tile([P, PACK, P], F32, name="diff")
@@ -265,12 +277,15 @@ def tile_lvq_t_v_kernel(tc, x, prototypes, dists, grad_out, out):
                 )
                 nc.sync.dma_start(out=out_view[:, i, cols], in_=result[:])
 
+        def vector_compares(i):
+            return i >= PASSES and i % 2 == 0
+
         def is_tile(i):
             return 0 <= i < TOKEN_TILES
 
-        load_dists(0)
-        load_grad_out(0)
+        load_dists(0, pieces=PASSES)
         load_prototypes(0)
+        load_grad_out(0)
         load_dists(1)
         for r in range(TOKEN_TILES + 5):
             if r + 1 < PASSES:
@@ -290,16 +305,15 @@ def tile_lvq_t_v_kernel(tc, x, prototypes, dists, grad_out, out):
                 mark_nearest(r - 1, 0)
                 mark_nearest(r - 1, 1)
             if is_tile(r):
-                find_minima(r)
-                if r >= PASSES:
+                find_minima(r, pieces=PASSES if r == 0 else 1)
+                if vector_compares(r):
                     compare_in_token_order(r, VECTOR_PASS)
-                negate_minima(r)
                 guess_reciprocal(r)
                 newton_products(r)
             if is_tile(r - 1):
                 transpose_differences(r - 1, 2)
                 mark_nearest(r - 1, 2)
-                if r - 1 >= PASSES:
+                if vector_compares(r - 1):
                     transpose_word_pairs(r - 1, VECTOR_PASS)
                     copy_word_pairs(r - 1, VECTOR_PASS)
                 else:

@@ -222,16 +222,15 @@ def tile_lvq_t_v_kernel(tc, x, prototypes, dists, grad_out, out):
             w_words = tiles["w_pairs", i][:].bitcast(F32)
             for s in range(PASSES):
                 nc.tensor.transpose(out=w_t[:, s, :], in_=w_words[:, s * P : (s + 1) * P], identity=ident[:])
-            w_t_sb = short.tile([P, PASSES * P], F32, name="w_t_sb")
-            nc.scalar.copy(out=w_t_sb[:], in_=w_t[:].rearrange("p s b -> p (s b)"))
-            tiles["w_t_sb", i] = w_t_sb
+            tiles["w_t", i] = w_t
 
         def scale_nearest(i):
             a_grouped = short.tile([P, PASSES * P * PACK], BF16, name="a_grouped", align_bytes=64)
             nc.vector.tensor_tensor(
                 out=a_grouped[:].rearrange("p (n u e) -> p n u e", u=2, e=2),
                 in0=tiles["near", i][:].rearrange("p s b (u e) -> p (s b) u e", u=2),
-                in1=tiles["w_t_sb", i][:]
+                in1=tiles["w_t", i][:]
+                .rearrange("p s b -> p (s b)")
                 .bitcast(BF16)
                 .rearrange("p (n o e) -> p n o e", o=1, e=2)
                 .to_broadcast([P, PASSES * P, 2, 2]),

from contextlib import ExitStack

import concourse.mybir as mybir
from concourse.masks import make_identity

F32 = mybir.dt.float32
BF16 = mybir.dt.bfloat16
U32 = mybir.dt.uint32
U8 = mybir.dt.uint8
E5M2_X4 = mybir.dt.float8_e5m2_x4
E4M3_X4 = mybir.dt.float8_e4m3fn_x4
ALU = mybir.AluOpType
ACT = mybir.ActivationFunctionType

P = 128
B = 2048
K = 2048
D = 1024
PPC = 8
C = K // PPC
PACK = 4
K_PASS = P * PACK
PASSES = K // K_PASS
N_TILE = 512
N_TILES = D // N_TILE
TOKEN_TILES = B // P
PREFETCH = 2
G_CHUNK = 4
STEEP = 2.0**60
VECTOR_PASS = 3

FLOPS = 2 * B * K * D


def tile_lvq_t_v_kernel(tc, x, prototypes, dists, grad_out, out):
    nc = tc.nc

    d_view = dists.rearrange("(p i) k -> p i k", i=TOKEN_TILES)
    g_view = grad_out.rearrange("(p i) c -> p i c", i=TOKEN_TILES)
    x_view = x.rearrange("(p i) d -> p i d", i=TOKEN_TILES)
    out_view = out.rearrange("(p i) d -> p i d", i=TOKEN_TILES)
    proto_view = prototypes.rearrange("(s p t) d -> s p t d", p=P, t=PACK)

    with ExitStack() as stack:
        keep = stack.enter_context(tc.tile_pool(name="keep", bufs=1))
        proto_pool = stack.enter_context(tc.tile_pool(name="proto", bufs=2))
        dist_pool = stack.enter_context(tc.tile_pool(name="dist", bufs=PREFETCH + 3))
        short = stack.enter_context(tc.tile_pool(name="short", bufs=3))
        x_pool = stack.enter_context(tc.tile_pool(name="x_pool", bufs=4))
        neg_r_pool = stack.enter_context(tc.tile_pool(name="neg_r", bufs=6))
        result_pool = stack.enter_context(tc.tile_pool(name="result", bufs=4))
        diff_pool = stack.enter_context(tc.psum_pool(name="diff", bufs=4))
        w_t_pool = stack.enter_context(tc.psum_pool(name="w_t", bufs=1))
        acc_pool = stack.enter_context(tc.psum_pool(name="acc", bufs=3))
        stack.enter_context(tc.manual_schedule())

        ident = keep.tile([P, P], F32)
        make_identity(nc, ident[:])
        g_sb = keep.tile([P, TOKEN_TILES, C], BF16)
        p_words = keep.tile([P, PASSES, D], U32, align_bytes=64)
        p_scales = keep.tile([P, PASSES, D], U8, align_bytes=64)
        tiles = {}

        def repeated(per_class, times):
            return per_class.rearrange("p (c o) -> p c o", o=1).to_broadcast([P, per_class.shape[1], times])

        def column_pieces(width, pieces):
            return [slice(j * width // pieces, (j + 1) * width // pieces) for j in range(pieces)]

        def load_dists(i, pieces=1):
            d_sb = dist_pool.tile([P, K], F32, name="d_sb")
            for cols in column_pieces(K, pieces):
                nc.sync.dma_start(out=d_sb[:, cols], in_=d_view[:, i, cols])
            tiles["d", i] = d_sb

        def load_grad_out(i):
            nc.sync.dma_start(out=g_sb[:, i : i + G_CHUNK, :], in_=g_view[:, i : i + G_CHUNK, :])

        def load_x(i):
            x_sb = x_pool.tile([P, D], BF16, name="x_sb")
            nc.sync.dma_start(out=x_sb[:], in_=x_view[:, i, :])
            tiles["x", i] = x_sb

        def load_prototypes(s):
            raw = proto_pool.tile([P, PACK, D], BF16, name="raw")
            for cols in column_pieces(D, N_TILES):
                nc.sync.dma_start(out=raw[:, :, cols], in_=proto_view[s][:, :, cols])
            tiles["raw", s] = raw

        def regroup_prototypes(s):
            grouped = proto_pool.tile([P, D, PACK], BF16, name="p_grouped", align_bytes=64)
            for n in range(N_TILES):
                cols = slice(n * N_TILE, (n + 1) * N_TILE)
                nc.vector.tensor_copy(out=grouped[:, cols, :], in_=tiles["raw", s][:, :, cols].rearrange("p t d -> p d t"))
            tiles["p_grouped", s] = grouped

        def quantise_prototypes(s):
            nc.vector.quantize_mx(
                out=p_words[:, s, :].bitcast(E4M3_X4),
                scales=p_scales[:, s, :],
                in_=tiles["p_grouped", s][:].rearrange("p d t -> p (d t)"),
            )

        def find_minima(i, pieces=1):
            m = short.tile([P, C], F32, name="m")
            neg_m = short.tile([P, 2 * C], F32, name="neg_m")
            for classes in column_pieces(C, pieces):
                nc.vector.tensor_reduce(
                    out=m[:, classes],
                    in_=tiles["d", i][:].rearrange("p (c j) -> p c j", j=PPC)[:, classes, :],
                    axis=mybir.AxisListType.X,
                    op=ALU.min,
                )
                nc.scalar.activation(
                    out=neg_m[:].rearrange("p (c v) -> p c v", v=2)[:, classes, :],
                    in_=repeated(m[:, classes], 2),
                    func=ACT.Copy,
                    scale=-1.0,
                )
            tiles["m", i] = m
            tiles["neg_m", i] = neg_m

        def guess_reciprocal(i):
            rsqrt_m = short.tile([P, C], F32, name="rsqrt_m")
            nc.scalar.activation(out=rsqrt_m[:], in_=tiles["m", i][:], func=ACT.Abs_reciprocal_sqrt)
            guess = short.tile([P, C], F32, name="guess")
            nc.scalar.activation(out=guess[:], in_=rsqrt_m[:], func=ACT.Square)
            tiles["guess", i] = guess

        def newton_products(i):
            m_guess = short.tile([P, C], F32, name="m_guess")
            nc.gpsimd.tensor_tensor(out=m_guess[:], in0=tiles["m", i][:], in1=tiles["guess", i][:], op=ALU.mult)
            w_guess = short.tile([P, C], F32, name="w_guess")
            nc.gpsimd.tensor_tensor(out=w_guess[:], in0=g_sb[:, i, :], in1=tiles["guess", i][:], op=ALU.mult)
            tiles["m_guess", i] = m_guess
            tiles["w_guess", i] = w_guess

        def newton_finish(i):
            neg_w = short.tile([P, C], F32, name="neg_w")
            nc.vector.scalar_tensor_tensor(
                out=neg_w[:],
                in0=tiles["m_guess", i][:],
                scalar=2.0,
                in1=tiles["w_guess", i][:],
                op0=ALU.subtract,
                op1=ALU.mult,
            )
            tiles["neg_w", i] = neg_w

        def round_weights(i):
            w_pairs = short.tile([P, 4 * C], BF16, name="w_pairs")
            four_r = short.tile([P, 1], F32, name="four_r")
            nc.scalar.activation(
                out=w_pairs[:].rearrange("p (c f) -> p c f", f=4),
                in_=repeated(tiles["neg_w", i][:], 4),
                func=ACT.Copy,
                scale=-1.0,
                accum_out=four_r[:],
            )
            neg_r = neg_r_pool.tile([P, 1], F32, name="neg_r")
            nc.scalar.mul(out=neg_r[:], in_=four_r[:], mul=-0.25)
            tiles["w_pairs", i] = w_pairs
            tiles["neg_r", i] = neg_r

        def transpose_differences(i, s):
            diff = diff_pool.tile([P, PACK, P], F32, name="diff")
            d_cols = tiles["d", i][:].rearrange("p (s q t) -> p s t q", s=PASSES, t=PACK)
            for t in range(PACK):
                nc.tensor.matmul(
                    out=diff[:, t, :], lhsT=d_cols[:, s, t, :], rhs=ident[:], start=True, stop=False, is_transpose=True
                )
                nc.tensor.matmul(
                    out=diff[:, t, :],
                    lhsT=tiles["neg_m", i][:, s * P : (s + 1) * P],
                    rhs=ident[:],
                    start=False,
                    stop=True,
                    is_transpose=True,
                )
            tiles["diff", i, s] = diff

        def compare_in_token_order(i, s):
            near_rows = short.tile([P, K_PASS], BF16, name="near_rows")
            classes = K_PASS // PPC
            nc.vector.tensor_tensor(
                out=near_rows[:].rearrange("p (c j) -> p c j", j=PPC),
                in0=tiles["d", i][:, s * K_PASS : (s + 1) * K_PASS].rearrange("p (c j) -> p c j", j=PPC),
                in1=tiles["m", i][:, s * classes : (s + 1) * classes]
                .rearrange("p (c o) -> p c o", o=1)
                .to_broadcast([P, classes, PPC]),
                op=ALU.is_equal,
            )
            tiles["near_rows", i] = near_rows

        def transpose_word_pairs(i, s):
            pairs = diff_pool.tile([P, 2, P], F32, name="diff")
            words = tiles["near_rows", i][:].bitcast(F32).rearrange("p (q u) -> p u q", u=2)
            for u in range(2):
                nc.tensor.transpose(out=pairs[:, u, :], in_=words[:, u, :], identity=ident[:])
            tiles["pairs", i, s] = pairs

        def copy_word_pairs(i, s):
            near_words = tiles["near", i][:].rearrange("p s b t -> p (s b t)").bitcast(F32)
            nc.scalar.copy(
                out=near_words.rearrange("p (s b u) -> p s b u", s=PASSES, u=2)[:, s, :, :],
                in_=tiles["pairs", i, s][:].rearrange("p u b -> p b u"),
            )

        def mark_nearest(i, s):
            if s == 0:
                tiles["near", i] = short.tile([P, PASSES, P, PACK], BF16, name="near")
            nc.scalar.activation(
                out=tiles["near", i][:, s, :, :],
                in_=tiles["diff", i, s][:].rearrange("p t b -> p b t"),
                func=ACT.Relu,
                scale=-STEEP,
                bias=1.0,
            )

        def transpose_weights(i):
            w_t = w_t_pool.tile([P, PASSES, P], F32, name="w_t")
            w_words = tiles["w_pairs", i][:].bitcast(F32)
            for s in range(PASSES):
                nc.tensor.transpose(out=w_t[:, s, :], in_=w_words[:, s * P : (s + 1) * P], identity=ident[:])
            tiles["w_t", i] = w_t

        def scale_nearest(i):
            a_grouped = short.tile([P, PASSES * P * PACK], BF16, name="a_grouped", align_bytes=64)
            nc.vector.tensor_tensor(
                out=a_grouped[:].rearrange("p (n u e) -> p n u e", u=2, e=2),
                in0=tiles["near", i][:].rearrange("p s b (u e) -> p (s b) u e", u=2),
                in1=tiles["w_t", i][:]
                .rearrange("p s b -> p (s b)")
                .bitcast(BF16)
                .rearrange("p (n o e) -> p n o e", o=1, e=2)
                .to_broadcast([P, PASSES * P, 2, 2]),
                op=ALU.mult,
            )
            tiles["a_grouped", i] = a_grouped

        def quantise_a(i):
            a_words = short.tile([P, PASSES * P], U32, name="a_words", align_bytes=64)
            a_scales = short.tile([P, PASSES * P], U8, name="a_scales", align_bytes=64)
            nc.vector.quantize_mx(out=a_words[:].bitcast(E5M2_X4), scales=a_scales[:], in_=tiles["a_grouped", i][:])
            tiles["a_words", i] = a_words
            tiles["a_scales", i] = a_scales

        def multiply(i):
            for n in range(N_TILES):
                cols = slice(n * N_TILE, (n + 1) * N_TILE)
                acc = acc_pool.tile([P, N_TILE], F32, name="acc")
                for s in range(PASSES):
                    tokens = slice(s * P, (s + 1) * P)
                    nc.tensor.matmul_mx(
                        out=acc[:],
                        lhsT=tiles["a_words", i][:, tokens].bitcast(E5M2_X4),
                        lhsT_scale=tiles["a_scales", i][:, tokens],
                        rhs=p_words[:, s, cols].bitcast(E4M3_X4),
                        rhs_scale=p_scales[:, s, cols],
                        start=(s == 0),
                        stop=(s == PASSES - 1),
                    )
                tiles["acc", i, n] = acc

        def subtract_and_store(i):
            for n in range(N_TILES):
                cols = slice(n * N_TILE, (n + 1) * N_TILE)
                result = result_pool.tile([P, N_TILE], F32, name="result")
                nc.vector.scalar_tensor_tensor(
                    out=result[:],
                    in0=tiles["x", i][:, cols],
                    scalar=tiles["neg_r", i][:, 0:1],
                    in1=tiles["acc", i, n][:],
                    op0=ALU.mult,
                    op1=ALU.add,
                )
                nc.sync.dma_start(out=out_view[:, i, cols], in_=result[:])

        def vector_compares(i):
            return i >= PASSES and i % 2 == 0

        def is_tile(i):
            return 0 <= i < TOKEN_TILES

        load_dists(0, pieces=PASSES)
        load_prototypes(0)
        load_grad_out(0)
        load_dists(1)
        for r in range(TOKEN_TILES + 5):
            if r + 1 < PASSES:
                load_prototypes(r + 1)
            if is_tile(r + PREFETCH):
                load_dists(r + PREFETCH)
            if is_tile(r + 1) and (r + 1) % G_CHUNK == 0:
                load_grad_out(r + 1)
            if is_tile(r - 3):
                load_x(r - 3)
            if is_tile(r - 2):
                newton_finish(r - 2)
                round_weights(r - 2)
            if is_tile(r - 1):
                transpose_differences(r - 1, 0)
                transpose_differences(r - 1, 1)
                mark_nearest(r - 1, 0)
                mark_nearest(r - 1, 1)
            if is_tile(r):
                find_minima(r, pieces=PASSES if r == 0 else 1)
                if vector_compares(r):
                    compare_in_token_order(r, VECTOR_PASS)
                guess_reciprocal(r)
                newton_products(r)
            if is_tile(r - 1):
                transpose_differences(r - 1, 2)
                mark_nearest(r - 1, 2)
                if vector_compares(r - 1):
                    transpose_word_pairs(r - 1, VECTOR_PASS)
                    copy_word_pairs(r - 1, VECTOR_PASS)
                else:
                    transpose_differences(r - 1, VECTOR_PASS)
                    mark_nearest(r - 1, VECTOR_PASS)
            if is_tile(r - 2):
                transpose_weights(r - 2)
            if r < PASSES:
                regroup_prototypes(r)
            if is_tile(r - 4):
                quantise_a(r - 4)
            if is_tile(r - 3):
                scale_nearest(r - 3)
            if is_tile(r - 5):
                subtract_and_store(r - 5)
            if r < PASSES:
                quantise_prototypes(r)
            if is_tile(r - 4):
                multiply(r - 4)
